import numpy as np
import ml_dtypes


def mxq(x, axis, fmt="e4m3"):
    dtype, down = {"e4m3": (ml_dtypes.float8_e4m3fn, 7), "e5m2": (ml_dtypes.float8_e5m2, 14)}[fmt]
    v = np.moveaxis(np.asarray(x, np.float32).astype(ml_dtypes.bfloat16).astype(np.float64), axis, -1)
    blocks = v.reshape(v.shape[:-1] + (-1, 32))
    amax = np.abs(blocks).max(-1, keepdims=True)
    byte = np.maximum(np.where(amax > 0, np.frexp(amax)[1] - 1 + 127, 0) - down, 1)
    scale = np.exp2(byte - 127.0)
    codes = (blocks / scale).astype(np.float32).astype(dtype).astype(np.float64)
    return np.moveaxis((codes * scale).reshape(v.shape), -1, axis)


WIDE = False


def mx_kscale(k):
    if not WIDE:
        return np.ones(k)
    levels = np.array([10, -10, 5, -5, 0])
    if k % 512:
        return np.exp2(np.random.permutation(np.resize(levels, k // 32))).repeat(32)
    a = np.empty((k // 512, 16))
    for p in range(k // 512):
        a[p, :8] = np.random.permutation(np.resize(levels, 8))
        for g in range(8):
            far = levels[np.abs(levels - a[p, g]) >= 10]
            a[p, g + 8] = far[np.random.randint(len(far))]
    return np.exp2(a.ravel()).repeat(32)


BF16 = ml_dtypes.bfloat16


def bf(x):
    return np.asarray(x, np.float32).astype(BF16)


def f64(x):
    return np.asarray(x).astype(np.float64)


B, C, CP, H, W, KW = 1, 512, 19, 48, 48, 7
PAD = KW // 2
BN_EPS = 1e-5


def pad_hw(v):
    return np.pad(v, ((0, 0), (0, 0), (PAD, PAD), (PAD, PAD)))


def setup_inputs():
    s, t = mx_kscale(C), mx_kscale(C)
    return {
        "x": bf(np.random.standard_normal((B, C, H, W))),
        "coarse_probs": bf(np.random.random((B, CP, H, W))),
        "sigma": bf(1.5 + 0.1 * np.random.standard_normal(1)),
        "w_feat": bf(np.random.standard_normal((C, C)) * 2.0 / np.sqrt(C) * t[:, None] / s[None, :]),
        "w_fuse": bf(np.random.standard_normal((C, C)) * 2.5 / np.sqrt(C) / t[None, :]),
        "bn_gamma": bf((1.0 + 0.1 * np.random.standard_normal(C)) * s),
        "bn_beta": bf(0.1 * np.random.standard_normal(C) * s),
        "bn_mean": bf(0.1 * np.random.standard_normal(C)),
        "bn_var": bf(np.random.random(C) + 0.5),
    }


def reference(x, coarse_probs, sigma, w_feat, w_fuse, bn_gamma, bn_beta, bn_mean, bn_var):
    x, p = f64(x), f64(coarse_probs)
    inv = 1.0 / np.sqrt(f64(bn_var) + BN_EPS)
    xn = (x - f64(bn_mean)[None, :, None, None]) * (inv * f64(bn_gamma))[None, :, None, None] + f64(bn_beta)[None, :, None, None]

    pp = pad_hw(p)
    dist_sq = np.stack([((pp[:, :, i:i + H, j:j + W] - p) ** 2).sum(axis=1) for i in range(KW) for j in range(KW)], axis=1)
    denom = 2.0 * np.maximum(f64(sigma)[0], 0.0) ** 2 + 1e-8
    a = np.exp(-dist_sq / denom)
    e = np.exp(a - a.max(axis=1, keepdims=True))
    affinity = e / e.sum(axis=1, keepdims=True)

    xq = mxq(xn, 1, "e4m3")
    messages = (mxq(f64(w_feat), 1, "e4m3") @ xq.reshape(B, C, H * W)).reshape(B, C, H, W)

    mp = pad_hw(messages)
    agg = np.zeros((B, C, H, W))
    for i in range(KW):
        for j in range(KW):
            agg = agg + mp[:, :, i:i + H, j:j + W] * affinity[:, i * KW + j][:, None]

    aq = mxq(agg, 1, "e4m3")
    refined = (mxq(f64(w_fuse), 1, "e4m3") @ aq.reshape(B, C, H * W)).reshape(B, C, H, W)
    return x + refined

@@ -1,0 +1,342 @@
+from contextlib import ExitStack
+
+import concourse.masks as masks
+import concourse.mybir as mybir
+
+F32 = mybir.dt.float32
+BF16 = mybir.dt.bfloat16
+U32 = mybir.dt.uint32
+U8 = mybir.dt.uint8
+I32 = mybir.dt.int32
+FP8X4 = mybir.dt.float8_e4m3fn_x4
+ALU = mybir.AluOpType
+ACT = mybir.ActivationFunctionType
+AX = mybir.AxisListType
+
+P = 128
+C = 512
+CP = 19
+IMG_W = 48
+HW = 2304
+KW = 7
+NOFF = 49
+PAIRS = 9
+PADM = 160
+ML = HW + 2 * PADM
+PADP = 4
+PL = HW + 2 * PADP
+MSG_DT = F32
+G_COUNT = 17
+FLOPS = 2 * 2 * C * C * HW + 2 * NOFF * C * HW + 3 * NOFF * CP * HW
+
+
+def tile_dcblock_kernel(tc, x, coarse_probs, sigma, w_feat, w_fuse, bn_gamma, bn_beta, bn_mean, bn_var, out):
+    nc = tc.nc
+    x_v = x[0].rearrange("(p j) h w -> p j (h w)", j=4)
+    out_v = out[0].rearrange("(m t) h w -> m t (h w)", t=4)
+    cp_v = coarse_probs[0].rearrange("c h w -> c (h w)")
+    g_set = set(i for i in range(NOFF) if ((i + 1) * G_COUNT) // NOFF > (i * G_COUNT) // NOFF)
+
+    with ExitStack() as ctx:
+        const = ctx.enter_context(tc.tile_pool(name="const", bufs=1))
+        work = ctx.enter_context(tc.tile_pool(name="work", bufs=2))
+        affp = ctx.enter_context(tc.tile_pool(name="affp", bufs=2))
+        accp = ctx.enter_context(tc.tile_pool(name="accp", bufs=4))
+        ps_win = ctx.enter_context(tc.psum_pool(name="ps_win", bufs=5))
+        ps_aux = ctx.enter_context(tc.psum_pool(name="ps_aux", bufs=3))
+
+        x_raw = const.tile([P, 4, HW], BF16, name="x_raw")
+        wf_raw = const.tile([P, 4, C], BF16, name="wf_raw")
+        wu_raw = const.tile([P, 4, C], BF16, name="wu_raw")
+        chunks = [(0, 512), (512, 512), (1024, 512), (1536, 512), (2048, 256)]
+        nc.sync.dma_start(out=x_raw[:, :, 0:512], in_=x_v[:, :, 0:512])
+        nc.sync.dma_start(out=wf_raw[:], in_=w_feat.rearrange("(m t) k -> m t k", t=4))
+        for c0, wd in chunks[1:]:
+            nc.sync.dma_start(out=x_raw[:, :, c0:c0 + wd], in_=x_v[:, :, c0:c0 + wd])
+        nc.sync.dma_start(out=wu_raw[:], in_=w_fuse.rearrange("(m t) k -> m t k", t=4))
+
+        gam = const.tile([P, 4], BF16, name="gam")
+        bet = const.tile([P, 4], BF16, name="bet")
+        mea = const.tile([P, 4], BF16, name="mea")
+        var = const.tile([P, 4], BF16, name="var")
+        sig = const.tile([P, 1], BF16, name="sig")
+        nc.scalar.dma_start(out=var[:], in_=bn_var.rearrange("(p j) -> p j", j=4))
+        nc.scalar.dma_start(out=gam[:], in_=bn_gamma.rearrange("(p j) -> p j", j=4))
+        nc.scalar.dma_start(out=mea[:], in_=bn_mean.rearrange("(p j) -> p j", j=4))
+        nc.scalar.dma_start(out=bet[:], in_=bn_beta.rearrange("(p j) -> p j", j=4))
+        nc.scalar.dma_start(out=sig[:], in_=sigma.partition_broadcast(P))
+
+        pk_a = const.tile([P, PL], BF16, name="pk_a")
+        pk_b = const.tile([P, PL], BF16, name="pk_b")
+        nc.vector.memset(pk_a[:], 0.0)
+        nc.gpsimd.memset(pk_b[:], 0.0)
+        for dix in range(KW):
+            di = dix - 3
+            pk = pk_a if dix < 4 else pk_b
+            s = dix if dix < 4 else dix - 4
+            q_lo = max(0, PADP - IMG_W * di)
+            q_hi = min(PL, HW + PADP - IMG_W * di)
+            nc.scalar.dma_start(
+                out=pk[CP * s:CP * s + CP, q_lo:q_hi],
+                in_=cp_v[:, q_lo - PADP + IMG_W * di:q_hi - PADP + IMG_W * di],
+            )
+
+        ident_f = const.tile([P, P], F32, name="ident_f")
+        masks.make_identity(nc, ident_f[:])
+        ident_b = const.tile([P, P], BF16, name="ident_b")
+        masks.make_identity(nc, ident_b[:])
+        ident_w = ident_f
+
+        msg = const.tile([P, 4, ML], MSG_DT, name="msg")
+        nc.gpsimd.memset(msg[:, :, 0:PADM], 0.0)
+        nc.gpsimd.memset(msg[:, :, PADM + HW:ML], 0.0)
+
+        v1 = const.tile([P, 4], F32, name="v1")
+        nc.vector.tensor_scalar_add(out=v1[:], in0=var[:], scalar1=1e-5)
+        sq = const.tile([P, 4], F32, name="sq")
+        nc.scalar.activation(out=sq[:], in_=v1[:], func=ACT.Sqrt)
+        r0 = const.tile([P, 4], F32, name="r0")
+        nc.vector.reciprocal(out=r0[:], in_=sq[:])
+        nt = const.tile([P, 4], F32, name="nt")
+        nc.vector.tensor_tensor(out=nt[:], in0=r0[:], in1=r0[:], op=ALU.mult)
+        nc.vector.tensor_tensor(out=nt[:], in0=nt[:], in1=v1[:], op=ALU.mult)
+        nc.vector.tensor_scalar(out=nt[:], in0=nt[:], scalar1=-0.5, scalar2=1.5, op0=ALU.mult, op1=ALU.add)
+        nc.vector.tensor_tensor(out=nt[:], in0=nt[:], in1=r0[:], op=ALU.mult)
+        bn_s = const.tile([P, 4], F32, name="bn_s")
+        nc.vector.tensor_tensor(out=bn_s[:], in0=nt[:], in1=gam[:], op=ALU.mult)
+        bn_b = const.tile([P, 4], F32, name="bn_b")
+        nc.vector.tensor_tensor(out=bn_b[:], in0=bn_s[:], in1=mea[:], op=ALU.mult)
+        nc.vector.tensor_tensor(out=bn_b[:], in0=bet[:], in1=bn_b[:], op=ALU.subtract)
+
+        sg = const.tile([P, 1], F32, name="sg")
+        nc.vector.tensor_scalar_max(out=sg[:], in0=sig[:], scalar1=0.0)
+        nc.vector.tensor_tensor(out=sg[:], in0=sg[:], in1=sg[:], op=ALU.mult)
+        nc.vector.tensor_scalar(out=sg[:], in0=sg[:], scalar1=2.0, scalar2=1e-8, op0=ALU.mult, op1=ALU.add)
+        neginv = const.tile([P, 1], F32, name="neginv")
+        nc.vector.reciprocal(out=neginv[:], in_=sg[:])
+        nc.vector.tensor_scalar_mul(out=neginv[:], in0=neginv[:], scalar1=-1.0)
+
+        NT = 2 * PAIRS
+        n_i = const.tile([P, NT], I32, name="n_i")
+        nc.gpsimd.iota(n_i[:], pattern=[[P, NT]], base=0, channel_multiplier=1)
+        thr_i = const.tile([P, IMG_W - 1], I32, name="thr_i")
+        nc.gpsimd.iota(thr_i[:], pattern=[[IMG_W, IMG_W - 1]], base=IMG_W, channel_multiplier=0)
+        dj_i = const.tile([P, KW], I32, name="dj_i")
+        nc.gpsimd.iota(dj_i[:], pattern=[[1, KW]], base=-3, channel_multiplier=0)
+        n_f = const.tile([P, NT], F32, name="n_f")
+        nc.vector.tensor_copy(out=n_f[:], in_=n_i[:])
+        thr_f = const.tile([P, IMG_W - 1], F32, name="thr_f")
+        nc.vector.tensor_copy(out=thr_f[:], in_=thr_i[:])
+        dj_f = const.tile([P, KW], F32, name="dj_f")
+        nc.vector.tensor_copy(out=dj_f[:], in_=dj_i[:])
+        cmp = const.tile([P, NT, IMG_W - 1], F32, name="cmp")
+        nc.vector.tensor_tensor(
+            out=cmp[:],
+            in0=n_f[:].unsqueeze(2).to_broadcast([P, NT, IMG_W - 1]),
+            in1=thr_f[:].unsqueeze(1).to_broadcast([P, NT, IMG_W - 1]),
+            op=ALU.is_ge,
+        )
+        row = const.tile([P, NT], F32, name="row")
+        nc.vector.tensor_reduce(out=row[:], in_=cmp[:], axis=AX.X, op=ALU.add)
+        col = const.tile([P, NT], F32, name="col")
+        nc.vector.scalar_tensor_tensor(out=col[:], in0=row[:], scalar=-48.0, in1=n_f[:], op0=ALU.mult, op1=ALU.add)
+        cj = const.tile([P, NT, KW], F32, name="cj")
+        nc.vector.tensor_tensor(
+            out=cj[:],
+            in0=col[:].unsqueeze(2).to_broadcast([P, NT, KW]),
+            in1=dj_f[:].unsqueeze(1).to_broadcast([P, NT, KW]),
+            op=ALU.add,
+        )
+        m_lo = const.tile([P, NT, KW], F32, name="m_lo")
+        nc.vector.tensor_scalar(out=m_lo[:], in0=cj[:], scalar1=0.0, scalar2=None, op0=ALU.is_ge)
+        mask7 = const.tile([P, NT, KW], F32, name="mask7")
+        nc.vector.scalar_tensor_tensor(
+            out=mask7[:].rearrange("p t j -> p (t j)"),
+            in0=cj[:].rearrange("p t j -> p (t j)"),
+            scalar=47.0,
+            in1=m_lo[:].rearrange("p t j -> p (t j)"),
+            op0=ALU.is_le,
+            op1=ALU.mult,
+        )
+        cnt = const.tile([P, NT], F32, name="cnt")
+        nc.vector.tensor_reduce(out=cnt[:], in_=mask7[:], axis=AX.X, op=ALU.add)
+        nc.vector.tensor_scalar(out=cnt[:], in0=cnt[:], scalar1=-7.0, scalar2=49.0, op0=ALU.mult, op1=ALU.add)
+        mask49 = const.tile([P, NT, KW, KW], F32, name="mask49")
+        nc.vector.tensor_copy(out=mask49[:], in_=mask7[:].unsqueeze(3).to_broadcast([P, NT, KW, KW]))
+
+        def prep_weight(raw, label):
+            grouped = const.tile([P, 4 * C], BF16, name=label + "_grouped", align_bytes=64)
+            gw = grouped[:].bitcast(F32).rearrange("p (t m u) -> p t m u", t=4, u=2)
+            for half in range(2):
+                ps = ps_aux.tile([P, 2, 2, P], F32, name=label + "_ps", tag="aux")
+                for tt in range(2):
+                    words = raw[:, 2 * half + tt, :].bitcast(F32)
+                    for u in range(2):
+                        nc.tensor.transpose(ps[:, tt, u, :], words[:, u::2], ident_f[:])
+                nc.vector.tensor_copy(out=gw[:, 2 * half:2 * half + 2], in_=ps[:].rearrange("p t u m -> p t m u"))
+            codes = const.tile([P, C], U32, name=label + "_codes", align_bytes=64)
+            scl = const.tile([P, C], U8, name=label + "_scl", align_bytes=64)
+            nc.vector.quantize_mx(out=codes[:].bitcast(FP8X4), scales=scl[:], in_=grouped[:])
+            return codes, scl
+
+        wf_codes, wf_scl = prep_weight(wf_raw, "wf")
+
+        x_codes = const.tile([P, HW], U32, name="x_codes", align_bytes=64)
+        x_scl = const.tile([P, HW], U8, name="x_scl", align_bytes=64)
+
+        def stage1(k):
+            c0, wd = chunks[k]
+            xn = work.tile([P, 4, wd], BF16, name="xn", tag="xn")
+            for j in range(4):
+                nc.scalar.activation(
+                    out=xn[:, j, :], in_=x_raw[:, j, c0:c0 + wd], func=ACT.Identity,
+                    scale=bn_s[:, j:j + 1], bias=bn_b[:, j:j + 1],
+                )
+            xg = work.tile([P, wd, 4], BF16, name="xg", tag="xg", align_bytes=64)
+            nc.vector.tensor_copy(out=xg[:], in_=xn[:].rearrange("p j n -> p n j"))
+            nc.vector.quantize_mx(
+                out=x_codes[:, c0:c0 + wd].bitcast(FP8X4), scales=x_scl[:, c0:c0 + wd],
+                in_=xg[:].rearrange("p n j -> p (n j)"),
+            )
+            for i in range(4 if wd == 512 else 2):
+                bank = ps_win.tile([P, 2, 256], MSG_DT, name="bank", tag="win")
+                for h in range(2):
+                    t = i if wd == 512 else 2 * i + h
+                    n0 = c0 + 256 * h if wd == 512 else c0
+                    nc.tensor.matmul_mx(
+                        out=bank[:, h, :],
+                        lhsT=wf_codes[:, P * t:P * t + P].bitcast(FP8X4), lhsT_scale=wf_scl[:, P * t:P * t + P],
+                        rhs=x_codes[:, n0:n0 + 256].bitcast(FP8X4), rhs_scale=x_scl[:, n0:n0 + 256],
+                        start=True, stop=True,
+                    )
+                if wd == 512:
+                    nc.scalar.copy(out=msg[:, i, PADM + c0:PADM + c0 + 512], in_=bank[:].rearrange("p h n -> p (h n)"))
+                else:
+                    nc.scalar.copy(out=msg[:, 2 * i:2 * i + 2, PADM + c0:PADM + c0 + 256], in_=bank[:])
+
+        def affinity(pi):
+            diff = affp.tile([P, 2, NOFF + 1, CP], F32, name="diff", tag="diff")
+            for a in range(2):
+                n0 = PADP + P * (2 * pi + a) - 3
+                win_a = ps_aux.tile([P, KW, P], BF16, name="win_a", tag="aux")
+                win_b = ps_aux.tile([P, KW, P], BF16, name="win_b", tag="aux")
+                for djx in range(KW):
+                    nc.tensor.transpose(win_a[:, djx, :], pk_a[:, n0 + djx:n0 + djx + P], ident_b[:])
+                for djx in range(KW):
+                    nc.tensor.transpose(win_b[:, djx, :], pk_b[:, n0 + djx:n0 + djx + P], ident_b[:])
+                nc.scalar.copy(out=diff[:, a, NOFF, :], in_=win_a[:, 3, 3 * CP:4 * CP])
+                dv = diff[:, a, 0:NOFF, :].rearrange("p (j i) c -> p j i c", i=KW)
+                centre = diff[:, a, NOFF:NOFF + 1, :].unsqueeze(1)
+                nc.vector.tensor_tensor(
+                    out=dv[:, :, 0:4, :], in0=win_a[:, :, 0:4 * CP].rearrange("p j (i c) -> p j i c", c=CP),
+                    in1=centre.to_broadcast([P, KW, 4, CP]), op=ALU.subtract,
+                )
+                nc.vector.tensor_tensor(
+                    out=dv[:, :, 4:7, :], in0=win_b[:, :, 0:3 * CP].rearrange("p j (i c) -> p j i c", c=CP),
+                    in1=centre.to_broadcast([P, KW, 3, CP]), op=ALU.subtract,
+                )
+            flat = diff[:].rearrange("p a f c -> p (a f c)")
+            nc.scalar.activation(out=flat, in_=flat, func=ACT.Square)
+            dist = affp.tile([P, 2 * (NOFF + 1)], F32, name="dist", tag="dist")
+            nc.vector.tensor_reduce(out=dist[:], in_=diff[:].rearrange("p a f c -> p (a f) c"), axis=AX.X, op=ALU.add)
+            gau = affp.tile([P, 2 * (NOFF + 1)], F32, name="gau", tag="gau")
+            nc.scalar.activation(out=gau[:], in_=dist[:], func=ACT.Exp, scale=neginv[:, 0:1])
+            ex = affp.tile([P, 2, NOFF + 1], F32, name="ex", tag="ex")
+            nc.scalar.activation(out=ex[:].rearrange("p a f -> p (a f)"), in_=gau[:], func=ACT.Exp, bias=-1.0)
+            em = affp.tile([P, 2, NOFF], F32, name="em", tag="em")
+            nc.vector.tensor_tensor(
+                out=em[:], in0=ex[:, :, 0:NOFF],
+                in1=mask49[:, 2 * pi:2 * pi + 2].rearrange("p t j i -> p t (j i)"), op=ALU.mult,
+            )
+            zs = affp.tile([P, 2], F32, name="zs", tag="zs")
+            nc.vector.tensor_reduce(out=zs[:], in_=em[:], axis=AX.X, op=ALU.add)
+            zo = affp.tile([P, 2], F32, name="zo", tag="zo")
+            nc.vector.tensor_tensor(out=zo[:], in0=ex[:, :, NOFF], in1=cnt[:, 2 * pi:2 * pi + 2], op=ALU.mult)
+            nc.vector.tensor_tensor(out=zo[:], in0=zo[:], in1=zs[:], op=ALU.add)
+            rz = affp.tile([P, 2], F32, name="rz", tag="rz")
+            nc.vector.reciprocal(out=rz[:], in_=zo[:])
+            wa = affp.tile([P, 2, NOFF], F32, name="wa", tag="wa", bufs=3)
+            nc.vector.tensor_tensor(out=wa[:], in0=em[:], in1=rz[:].unsqueeze(2).to_broadcast([P, 2, NOFF]), op=ALU.mult)
+            return wa
+
+        def aggregate(pi, wa):
+            acc_v0 = accp.tile([P, C], F32, name="acc_v0", tag="acc_v")
+            acc_v1 = accp.tile([P, C], F32, name="acc_v1", tag="acc_v")
+            acc_g0 = accp.tile([P, C], F32, name="acc_g0", tag="acc_g")
+            acc_g1 = accp.tile([P, C], F32, name="acc_g1", tag="acc_g")
+            acc_v = [acc_v0, acc_v1]
+            acc_g = [acc_g0, acc_g1]
+            seen_v = 0
+            seen_g = 0
+            for f in range(NOFF):
+                djx, dix = divmod(f, KW)
+                shift = IMG_W * (dix - 3) + (djx - 3)
+                for a in range(2):
+                    base = PADM + P * (2 * pi + a) + shift
+                    win = ps_win.tile([P, C], MSG_DT, name="win", tag="win")
+                    for t in range(4):
+                        nc.tensor.transpose(win[:, P * t:P * t + P], msg[:, t, base:base + P], ident_w[:])
+                    wcol = wa[:, a, f:f + 1]
+                    if f in g_set:
+                        if seen_g == 0:
+                            nc.scalar.activation(out=acc_g[a][:], in_=win[:], func=ACT.Copy, scale=wcol)
+                        else:
+                            prod = accp.tile([P, C], F32, name="prod", tag="prod")
+                            nc.scalar.activation(out=prod[:], in_=win[:], func=ACT.Copy, scale=wcol)
+                            nc.gpsimd.tensor_tensor(out=acc_g[a][:], in0=acc_g[a][:], in1=prod[:], op=ALU.add)
+                    else:
+                        if seen_v == 0:
+                            nc.vector.tensor_scalar(out=acc_v[a][:], in0=win[:], scalar1=wcol, scalar2=None, op0=ALU.mult)
+                        else:
+                            nc.vector.scalar_tensor_tensor(
+                                out=acc_v[a][:], in0=win[:], scalar=wcol, in1=acc_v[a][:], op0=ALU.mult, op1=ALU.add,
+                            )
+                if f in g_set:
+                    seen_g += 1
+                else:
+                    seen_v += 1
+            agg_t = work.tile([P, 2, C], BF16, name="agg_t", tag="agg_t")
+            for a in range(2):
+                nc.gpsimd.tensor_tensor(out=agg_t[:, a, :], in0=acc_g[a][:], in1=acc_v[a][:], op=ALU.add)
+            return agg_t
+
+        def stage2(pi, agg_t):
+            back = ps_aux.tile([P, 2, 4, P], BF16, name="back", tag="aux")
+            for a in range(2):
+                for t in range(4):
+                    nc.tensor.transpose(back[:, a, t, :], agg_t[:, a, P * t:P * t + P], ident_b[:])
+            ag = work.tile([P, 2 * P, 4], BF16, name="ag", tag="ag", align_bytes=64)
+            nc.scalar.copy(out=ag[:].rearrange("p (a n) t -> p a n t", a=2), in_=back[:].rearrange("p a t n -> p a n t"))
+            a_codes = work.tile([P, 2 * P], U32, name="a_codes", tag="a_codes", align_bytes=64)
+            a_scl = work.tile([P, 2 * P], U8, name="a_scl", tag="a_scl", align_bytes=64)
+            nc.vector.quantize_mx(out=a_codes[:].bitcast(FP8X4), scales=a_scl[:], in_=ag[:].rearrange("p n t -> p (n t)"))
+            o_sb = work.tile([P, 4, 2 * P], F32, name="o_sb", tag="o_sb", bufs=3)
+            n0 = 2 * P * pi
+            for u in range(2):
+                ps2 = ps_aux.tile([P, 2, 2 * P], F32, name="ps2", tag="aux")
+                for h in range(2):
+                    t = 2 * u + h
+                    nc.tensor.matmul_mx(
+                        out=ps2[:, h, :],
+                        lhsT=wu_codes[:, P * t:P * t + P].bitcast(FP8X4), lhsT_scale=wu_scl[:, P * t:P * t + P],
+                        rhs=a_codes[:].bitcast(FP8X4), rhs_scale=a_scl[:],
+                        start=True, stop=True,
+                    )
+                nc.vector.tensor_tensor(
+                    out=o_sb[:, 2 * u:2 * u + 2, :], in0=ps2[:], in1=x_raw[:, 2 * u:2 * u + 2, n0:n0 + 2 * P], op=ALU.add,
+                )
+            nc.sync.dma_start(out=out_v[:, :, n0:n0 + 2 * P], in_=o_sb[:])
+
+        stage1(0)
+        wa_next = affinity(0)
+        stage1(1)
+        wu_codes, wu_scl = prep_weight(wu_raw, "wu")
+        need = {1: 2, 3: 3, 5: 4}
+        for pi in range(PAIRS):
+            wa_now = wa_next
+            if pi in need:
+                stage1(need[pi])
+            if pi + 1 < PAIRS:
+                wa_next = affinity(pi + 1)
+            agg_t = aggregate(pi, wa_now)
+            stage2(pi, agg_t)

@@ -27,6 +27,7 @@ PADP = 4
 PL = HW + 2 * PADP
 MSG_DT = F32
 G_COUNT = 17
+X_COUNT = 1
 FLOPS = 2 * 2 * C * C * HW + 2 * NOFF * C * HW + 3 * NOFF * CP * HW
 
 
@@ -36,6 +37,8 @@ def tile_dcblock_kernel(tc, x, coarse_probs, sigma, w_feat, w_fuse, bn_gamma, bn
     out_v = out[0].rearrange("(m t) h w -> m t (h w)", t=4)
     cp_v = coarse_probs[0].rearrange("c h w -> c (h w)")
     g_set = set(i for i in range(NOFF) if ((i + 1) * G_COUNT) // NOFF > (i * G_COUNT) // NOFF)
+    rest = [i for i in range(NOFF) if i not in g_set]
+    x_set = set(rest[j] for j in range(len(rest)) if ((j + 1) * X_COUNT) // len(rest) > (j * X_COUNT) // len(rest))
 
     with ExitStack() as ctx:
         const = ctx.enter_context(tc.tile_pool(name="const", bufs=1))
@@ -49,12 +52,13 @@ def tile_dcblock_kernel(tc, x, coarse_probs, sigma, w_feat, w_fuse, bn_gamma, bn
         wf_raw = const.tile([P, 4, C], BF16, name="wf_raw")
         wu_raw = const.tile([P, 4, C], BF16, name="wu_raw")
         chunks = [(0, 512), (512, 512), (1024, 512), (1536, 512), (2048, 256)]
-        nc.sync.dma_start(out=x_raw[:, :, 0:512], in_=x_v[:, :, 0:512])
-        nc.sync.dma_start(out=wf_raw[:], in_=w_feat.rearrange("(m t) k -> m t k", t=4))
-        for c0, wd in chunks[1:]:
-            nc.sync.dma_start(out=x_raw[:, :, c0:c0 + wd], in_=x_v[:, :, c0:c0 + wd])
-        nc.sync.dma_start(out=wu_raw[:], in_=w_fuse.rearrange("(m t) k -> m t k", t=4))
 
+        pk_a = const.tile([P, PL], BF16, name="pk_a")
+        pk_b = const.tile([P, PL], BF16, name="pk_b")
+        one = const.tile([P, 1], F32, name="one")
+        nc.vector.memset(one[:], 1.0)
+        nc.vector.memset(pk_a[:], 0.0)
+        nc.gpsimd.memset(pk_b[:], 0.0)
         gam = const.tile([P, 4], BF16, name="gam")
         bet = const.tile([P, 4], BF16, name="bet")
         mea = const.tile([P, 4], BF16, name="mea")
@@ -66,20 +70,24 @@ def tile_dcblock_kernel(tc, x, coarse_probs, sigma, w_feat, w_fuse, bn_gamma, bn
         nc.scalar.dma_start(out=bet[:], in_=bn_beta.rearrange("(p j) -> p j", j=4))
         nc.scalar.dma_start(out=sig[:], in_=sigma.partition_broadcast(P))
 
-        pk_a = const.tile([P, PL], BF16, name="pk_a")
-        pk_b = const.tile([P, PL], BF16, name="pk_b")
-        nc.vector.memset(pk_a[:], 0.0)
-        nc.gpsimd.memset(pk_b[:], 0.0)
+        warm = const.tile([P, 1], F32, name="warm")
+        nc.scalar.activation(out=warm[:], in_=one[:], func=ACT.Sqrt)
         for dix in range(KW):
             di = dix - 3
             pk = pk_a if dix < 4 else pk_b
             s = dix if dix < 4 else dix - 4
             q_lo = max(0, PADP - IMG_W * di)
             q_hi = min(PL, HW + PADP - IMG_W * di)
-            nc.scalar.dma_start(
-                out=pk[CP * s:CP * s + CP, q_lo:q_hi],
-                in_=cp_v[:, q_lo - PADP + IMG_W * di:q_hi - PADP + IMG_W * di],
-            )
+            n_lo = q_lo - PADP + IMG_W * di
+            n_hi = q_hi - PADP + IMG_W * di
+            nc.sync.dma_start(out=pk[CP * s:CP * s + 16, q_lo:q_hi], in_=cp_v[0:16, n_lo:n_hi])
+            nc.scalar.dma_start(out=pk[CP * s + 16:CP * s + CP, q_lo:q_hi], in_=cp_v[16:CP, n_lo:n_hi])
+
+        nc.sync.dma_start(out=x_raw[:, :, 0:512], in_=x_v[:, :, 0:512])
+        nc.sync.dma_start(out=wf_raw[:], in_=w_feat.rearrange("(m t) k -> m t k", t=4))
+        for c0, wd in chunks[1:]:
+            nc.sync.dma_start(out=x_raw[:, :, c0:c0 + wd], in_=x_v[:, :, c0:c0 + wd])
+        nc.sync.dma_start(out=wu_raw[:], in_=w_fuse.rearrange("(m t) k -> m t k", t=4))
 
         ident_f = const.tile([P, P], F32, name="ident_f")
         masks.make_identity(nc, ident_f[:])
@@ -87,14 +95,15 @@ def tile_dcblock_kernel(tc, x, coarse_probs, sigma, w_feat, w_fuse, bn_gamma, bn
         masks.make_identity(nc, ident_b[:])
         ident_w = ident_f
 
-        msg = const.tile([P, 4, ML], MSG_DT, name="msg")
-        nc.gpsimd.memset(msg[:, :, 0:PADM], 0.0)
-        nc.gpsimd.memset(msg[:, :, PADM + HW:ML], 0.0)
+        msg = const.tile([P, 2, 4, ML // 2], MSG_DT, name="msg")
+        nc.gpsimd.memset(msg[:, :, :, 0:PADM // 2], 0.0)
+        nc.gpsimd.memset(msg[:, :, :, (PADM + HW) // 2:ML // 2], 0.0)
 
         v1 = const.tile([P, 4], F32, name="v1")
         nc.vector.tensor_scalar_add(out=v1[:], in0=var[:], scalar1=1e-5)
         sq = const.tile([P, 4], F32, name="sq")
         nc.scalar.activation(out=sq[:], in_=v1[:], func=ACT.Sqrt)
+        nc.scalar.activation(out=warm[:], in_=one[:], func=ACT.Exp)
         r0 = const.tile([P, 4], F32, name="r0")
         nc.vector.reciprocal(out=r0[:], in_=sq[:])
         nt = const.tile([P, 4], F32, name="nt")
@@ -118,7 +127,7 @@ def tile_dcblock_kernel(tc, x, coarse_probs, sigma, w_feat, w_fuse, bn_gamma, bn
 
         NT = 2 * PAIRS
         n_i = const.tile([P, NT], I32, name="n_i")
-        nc.gpsimd.iota(n_i[:], pattern=[[P, NT]], base=0, channel_multiplier=1)
+        nc.gpsimd.iota(n_i[:], pattern=[[2 * P, PAIRS], [1, 2]], base=0, channel_multiplier=2)
         thr_i = const.tile([P, IMG_W - 1], I32, name="thr_i")
         nc.gpsimd.iota(thr_i[:], pattern=[[IMG_W, IMG_W - 1]], base=IMG_W, channel_multiplier=0)
         dj_i = const.tile([P, KW], I32, name="dj_i")
@@ -186,14 +195,23 @@ def tile_dcblock_kernel(tc, x, coarse_probs, sigma, w_feat, w_fuse, bn_gamma, bn
 
         def stage1(k):
             c0, wd = chunks[k]
-            xn = work.tile([P, 4, wd], BF16, name="xn", tag="xn")
+            xn = work.tile([P, 4, wd], BF16, name="xn", tag="xn", bufs=1)
+            xg = work.tile([P, wd, 4], BF16, name="xg", tag="xg", align_bytes=64, bufs=1)
             for j in range(4):
-                nc.scalar.activation(
-                    out=xn[:, j, :], in_=x_raw[:, j, c0:c0 + wd], func=ACT.Identity,
-                    scale=bn_s[:, j:j + 1], bias=bn_b[:, j:j + 1],
-                )
-            xg = work.tile([P, wd, 4], BF16, name="xg", tag="xg", align_bytes=64)
-            nc.vector.tensor_copy(out=xg[:], in_=xn[:].rearrange("p j n -> p n j"))
+                if k == 0:
+                    nc.vector.tensor_scalar(
+                        out=xn[:, j, :], in0=x_raw[:, j, c0:c0 + wd],
+                        scalar1=bn_s[:, j:j + 1], scalar2=bn_b[:, j:j + 1], op0=ALU.mult, op1=ALU.add,
+                    )
+                else:
+                    nc.scalar.activation(
+                        out=xn[:, j, :], in_=x_raw[:, j, c0:c0 + wd], func=ACT.Identity,
+                        scale=bn_s[:, j:j + 1], bias=bn_b[:, j:j + 1],
+                    )
+            if k == 0:
+                nc.vector.tensor_copy(out=xg[:], in_=xn[:].rearrange("p j n -> p n j"))
+            else:
+                nc.scalar.copy(out=xg[:], in_=xn[:].rearrange("p j n -> p n j"))
             nc.vector.quantize_mx(
                 out=x_codes[:, c0:c0 + wd].bitcast(FP8X4), scales=x_scl[:, c0:c0 + wd],
                 in_=xg[:].rearrange("p n j -> p (n j)"),
@@ -210,20 +228,27 @@ def tile_dcblock_kernel(tc, x, coarse_probs, sigma, w_feat, w_fuse, bn_gamma, bn
                         start=True, stop=True,
                     )
                 if wd == 512:
-                    nc.scalar.copy(out=msg[:, i, PADM + c0:PADM + c0 + 512], in_=bank[:].rearrange("p h n -> p (h n)"))
+                    for e in range(2):
+                        nc.scalar.copy(
+                            out=msg[:, e, i, (PADM + c0) // 2:(PADM + c0) // 2 + 256],
+                            in_=bank[:].rearrange("p h n -> p (h n)")[:, e::2],
+                        )
                 else:
-                    nc.scalar.copy(out=msg[:, 2 * i:2 * i + 2, PADM + c0:PADM + c0 + 256], in_=bank[:])
+                    for e in range(2):
+                        nc.scalar.copy(
+                            out=msg[:, e, 2 * i:2 * i + 2, (PADM + c0) // 2:(PADM + c0) // 2 + P], in_=bank[:, :, e::2],
+                        )
 
         def affinity(pi):
             diff = affp.tile([P, 2, NOFF + 1, CP], F32, name="diff", tag="diff")
             for a in range(2):
-                n0 = PADP + P * (2 * pi + a) - 3
+                n0 = PADP + 2 * P * pi + a - 3
                 win_a = ps_aux.tile([P, KW, P], BF16, name="win_a", tag="aux")
                 win_b = ps_aux.tile([P, KW, P], BF16, name="win_b", tag="aux")
                 for djx in range(KW):
-                    nc.tensor.transpose(win_a[:, djx, :], pk_a[:, n0 + djx:n0 + djx + P], ident_b[:])
+                    nc.tensor.transpose(win_a[:, djx, :], pk_a[:, n0 + djx:n0 + djx + 2 * P:2], ident_b[:])
                 for djx in range(KW):
-                    nc.tensor.transpose(win_b[:, djx, :], pk_b[:, n0 + djx:n0 + djx + P], ident_b[:])
+                    nc.tensor.transpose(win_b[:, djx, :], pk_b[:, n0 + djx:n0 + djx + 2 * P:2], ident_b[:])
                 nc.scalar.copy(out=diff[:, a, NOFF, :], in_=win_a[:, 3, 3 * CP:4 * CP])
                 dv = diff[:, a, 0:NOFF, :].rearrange("p (j i) c -> p j i c", i=KW)
                 centre = diff[:, a, NOFF:NOFF + 1, :].unsqueeze(1)
@@ -244,73 +269,91 @@ def tile_dcblock_kernel(tc, x, coarse_probs, sigma, w_feat, w_fuse, bn_gamma, bn
             ex = affp.tile([P, 2, NOFF + 1], F32, name="ex", tag="ex")
             nc.scalar.activation(out=ex[:].rearrange("p a f -> p (a f)"), in_=gau[:], func=ACT.Exp, bias=-1.0)
             em = affp.tile([P, 2, NOFF], F32, name="em", tag="em")
-            nc.vector.tensor_tensor(
+            nc.gpsimd.tensor_tensor(
                 out=em[:], in0=ex[:, :, 0:NOFF],
                 in1=mask49[:, 2 * pi:2 * pi + 2].rearrange("p t j i -> p t (j i)"), op=ALU.mult,
             )
             zs = affp.tile([P, 2], F32, name="zs", tag="zs")
             nc.vector.tensor_reduce(out=zs[:], in_=em[:], axis=AX.X, op=ALU.add)
             zo = affp.tile([P, 2], F32, name="zo", tag="zo")
-            nc.vector.tensor_tensor(out=zo[:], in0=ex[:, :, NOFF], in1=cnt[:, 2 * pi:2 * pi + 2], op=ALU.mult)
-            nc.vector.tensor_tensor(out=zo[:], in0=zo[:], in1=zs[:], op=ALU.add)
+            for a in range(2):
+                nc.scalar.activation(
+                    out=zo[:, a:a + 1], in_=ex[:, a, NOFF:NOFF + 1], func=ACT.Identity,
+                    scale=cnt[:, 2 * pi + a:2 * pi + a + 1], bias=zs[:, a:a + 1],
+                )
             rz = affp.tile([P, 2], F32, name="rz", tag="rz")
             nc.vector.reciprocal(out=rz[:], in_=zo[:])
             wa = affp.tile([P, 2, NOFF], F32, name="wa", tag="wa", bufs=3)
-            nc.vector.tensor_tensor(out=wa[:], in0=em[:], in1=rz[:].unsqueeze(2).to_broadcast([P, 2, NOFF]), op=ALU.mult)
+            for a in range(2):
+                nc.scalar.activation(out=wa[:, a, :], in_=em[:, a, :], func=ACT.Copy, scale=rz[:, a:a + 1])
             return wa
 
-        def aggregate(pi, wa):
-            acc_v0 = accp.tile([P, C], F32, name="acc_v0", tag="acc_v")
-            acc_v1 = accp.tile([P, C], F32, name="acc_v1", tag="acc_v")
-            acc_g0 = accp.tile([P, C], F32, name="acc_g0", tag="acc_g")
-            acc_g1 = accp.tile([P, C], F32, name="acc_g1", tag="acc_g")
-            acc_v = [acc_v0, acc_v1]
+        def aggregate(pi, wa, hooks):
+            acc_v = accp.tile([P, 2, C], F32, name="acc_v", tag="acc_v", bufs=3)
+            acc_g0 = accp.tile([P, 2, C], F32, name="acc_g0", tag="acc_g")
+            acc_g1 = accp.tile([P, 2, C], F32, name="acc_g1", tag="acc_g")
             acc_g = [acc_g0, acc_g1]
+            parts = []
             seen_v = 0
             seen_g = 0
             for f in range(NOFF):
+                for hook in hooks.get(f, []):
+                    hook()
                 djx, dix = divmod(f, KW)
                 shift = IMG_W * (dix - 3) + (djx - 3)
+                if f in x_set:
+                    prod = accp.tile([P, 2, C], F32, name="xprod", tag="xprod", bufs=8)
+                    parts.append(prod)
+                if f in g_set:
+                    if seen_g < 2:
+                        prod = acc_g[seen_g]
+                    else:
+                        prod = accp.tile([P, 2, C], F32, name="prod", tag="prod", bufs=3)
                 for a in range(2):
-                    base = PADM + P * (2 * pi + a) + shift
+                    base = PADM + 2 * P * pi + a + shift
                     win = ps_win.tile([P, C], MSG_DT, name="win", tag="win")
                     for t in range(4):
-                        nc.tensor.transpose(win[:, P * t:P * t + P], msg[:, t, base:base + P], ident_w[:])
+                        nc.tensor.transpose(win[:, P * t:P * t + P], msg[:, base % 2, t, base // 2:base // 2 + P], ident_w[:])
                     wcol = wa[:, a, f:f + 1]
-                    if f in g_set:
-                        if seen_g == 0:
-                            nc.scalar.activation(out=acc_g[a][:], in_=win[:], func=ACT.Copy, scale=wcol)
-                        else:
-                            prod = accp.tile([P, C], F32, name="prod", tag="prod")
-                            nc.scalar.activation(out=prod[:], in_=win[:], func=ACT.Copy, scale=wcol)
-                            nc.gpsimd.tensor_tensor(out=acc_g[a][:], in0=acc_g[a][:], in1=prod[:], op=ALU.add)
+                    if f in g_set or f in x_set:
+                        nc.scalar.activation(out=prod[:, a, :], in_=win[:], func=ACT.Copy, scale=wcol)
+                    elif seen_v == 0:
+                        nc.vector.tensor_scalar(out=acc_v[:, a, :], in0=win[:], scalar1=wcol, scalar2=None, op0=ALU.mult)
                     else:
-                        if seen_v == 0:
-                            nc.vector.tensor_scalar(out=acc_v[a][:], in0=win[:], scalar1=wcol, scalar2=None, op0=ALU.mult)
-                        else:
-                            nc.vector.scalar_tensor_tensor(
-                                out=acc_v[a][:], in0=win[:], scalar=wcol, in1=acc_v[a][:], op0=ALU.mult, op1=ALU.add,
-                            )
+                        nc.vector.scalar_tensor_tensor(
+                            out=acc_v[:, a, :], in0=win[:], scalar=wcol, in1=acc_v[:, a, :], op0=ALU.mult, op1=ALU.add,
+                        )
                 if f in g_set:
+                    if seen_g >= 2:
+                        tgt = acc_g[seen_g % 2]
+                        nc.gpsimd.tensor_tensor(out=tgt[:], in0=tgt[:], in1=prod[:], op=ALU.add)
                     seen_g += 1
-                else:
+                elif f not in x_set:
                     seen_v += 1
-            agg_t = work.tile([P, 2, C], BF16, name="agg_t", tag="agg_t")
-            for a in range(2):
-                nc.gpsimd.tensor_tensor(out=agg_t[:, a, :], in0=acc_g[a][:], in1=acc_v[a][:], op=ALU.add)
-            return agg_t
+            return parts + [acc_g0, acc_g1, acc_v]
 
-        def stage2(pi, agg_t):
-            back = ps_aux.tile([P, 2, 4, P], BF16, name="back", tag="aux")
-            for a in range(2):
-                for t in range(4):
-                    nc.tensor.transpose(back[:, a, t, :], agg_t[:, a, P * t:P * t + P], ident_b[:])
-            ag = work.tile([P, 2 * P, 4], BF16, name="ag", tag="ag", align_bytes=64)
-            nc.scalar.copy(out=ag[:].rearrange("p (a n) t -> p a n t", a=2), in_=back[:].rearrange("p a t n -> p a n t"))
+        def turn_back(parts, held, a, t):
+            if a == 0 and t == 0:
+                held["ag"] = work.tile([P, 2 * P, 4], BF16, name="ag", tag="ag", align_bytes=64)
+            if t == 0:
+                held["back"] = ps_aux.tile([P, 4, P], F32, name="back", tag="aux")
+            back = held["back"]
+            for i in range(len(parts)):
+                nc.tensor.matmul(
+                    out=back[:, t, :], lhsT=parts[i][:, a, P * t:P * t + P], rhs=ident_f[:],
+                    is_transpose=True, start=(i == 0), stop=(i == len(parts) - 1),
+                )
+            if t == 3:
+                nc.scalar.copy(
+                    out=held["ag"][:].rearrange("p (n a) t -> p a n t", a=2)[:, a], in_=back[:].rearrange("p t n -> p n t"),
+                )
+
+        def stage2(pi, held):
+            ag = held["ag"]
             a_codes = work.tile([P, 2 * P], U32, name="a_codes", tag="a_codes", align_bytes=64)
             a_scl = work.tile([P, 2 * P], U8, name="a_scl", tag="a_scl", align_bytes=64)
             nc.vector.quantize_mx(out=a_codes[:].bitcast(FP8X4), scales=a_scl[:], in_=ag[:].rearrange("p n t -> p (n t)"))
-            o_sb = work.tile([P, 4, 2 * P], F32, name="o_sb", tag="o_sb", bufs=3)
+            o_sb = work.tile([P, 4, 2 * P], F32, name="o_sb", tag="o_sb")
             n0 = 2 * P * pi
             for u in range(2):
                 ps2 = ps_aux.tile([P, 2, 2 * P], F32, name="ps2", tag="aux")
@@ -318,7 +361,7 @@ def tile_dcblock_kernel(tc, x, coarse_probs, sigma, w_feat, w_fuse, bn_gamma, bn
                     t = 2 * u + h
                     nc.tensor.matmul_mx(
                         out=ps2[:, h, :],
-                        lhsT=wu_codes[:, P * t:P * t + P].bitcast(FP8X4), lhsT_scale=wu_scl[:, P * t:P * t + P],
+                        lhsT=later["wu"][0][:, P * t:P * t + P].bitcast(FP8X4), lhsT_scale=later["wu"][1][:, P * t:P * t + P],
                         rhs=a_codes[:].bitcast(FP8X4), rhs_scale=a_scl[:],
                         start=True, stop=True,
                     )
@@ -327,16 +370,34 @@ def tile_dcblock_kernel(tc, x, coarse_probs, sigma, w_feat, w_fuse, bn_gamma, bn
                 )
             nc.sync.dma_start(out=out_v[:, :, n0:n0 + 2 * P], in_=o_sb[:])
 
+        later = {}
+
+        def make_weights():
+            later["wu"] = prep_weight(wu_raw, "wu")
+
+        def make_affinity(pi):
+            later["wa"] = affinity(pi)
+
         stage1(0)
-        wa_next = affinity(0)
-        stage1(1)
-        wu_codes, wu_scl = prep_weight(wu_raw, "wu")
-        need = {1: 2, 3: 3, 5: 4}
+        make_affinity(0)
+        before = None
         for pi in range(PAIRS):
-            wa_now = wa_next
-            if pi in need:
-                stage1(need[pi])
+            wa_now = later["wa"]
+            hooks = {}
+            if pi == 0:
+                hooks[4] = [lambda: stage1(1)]
+                hooks[10] = [make_weights]
+            if pi in (1, 3, 5):
+                hooks[18] = [lambda k=(pi + 3) // 2: stage1(k)]
+            if before is not None:
+                held = {}
+                for i in range(8):
+                    hooks[2 * i + 1] = [lambda pp=before, hh=held, a=i // 4, t=i % 4: turn_back(pp, hh, a, t)]
+                hooks[17] = [lambda q=pi - 1, hh=held: stage2(q, hh)]
             if pi + 1 < PAIRS:
-                wa_next = affinity(pi + 1)
-            agg_t = aggregate(pi, wa_now)
-            stage2(pi, agg_t)
+                hooks[20] = [lambda q=pi + 1: make_affinity(q)]
+            before = aggregate(pi, wa_now, hooks)
+        held = {}
+        for i in range(8):
+            turn_back(before, held, i // 4, i % 4)
+        stage2(PAIRS - 1, held)

from contextlib import ExitStack

import concourse.masks as masks
import concourse.mybir as mybir

F32 = mybir.dt.float32
BF16 = mybir.dt.bfloat16
U32 = mybir.dt.uint32
U8 = mybir.dt.uint8
I32 = mybir.dt.int32
FP8X4 = mybir.dt.float8_e4m3fn_x4
ALU = mybir.AluOpType
ACT = mybir.ActivationFunctionType
AX = mybir.AxisListType

P = 128
C = 512
CP = 19
IMG_W = 48
HW = 2304
KW = 7
NOFF = 49
PAIRS = 9
PADM = 160
ML = HW + 2 * PADM
PADP = 4
PL = HW + 2 * PADP
MSG_DT = F32
G_COUNT = 17
X_COUNT = 1
FLOPS = 2 * 2 * C * C * HW + 2 * NOFF * C * HW + 3 * NOFF * CP * HW


def tile_dcblock_kernel(tc, x, coarse_probs, sigma, w_feat, w_fuse, bn_gamma, bn_beta, bn_mean, bn_var, out):
    nc = tc.nc
    x_v = x[0].rearrange("(p j) h w -> p j (h w)", j=4)
    out_v = out[0].rearrange("(m t) h w -> m t (h w)", t=4)
    cp_v = coarse_probs[0].rearrange("c h w -> c (h w)")
    g_set = set(i for i in range(NOFF) if ((i + 1) * G_COUNT) // NOFF > (i * G_COUNT) // NOFF)
    rest = [i for i in range(NOFF) if i not in g_set]
    x_set = set(rest[j] for j in range(len(rest)) if ((j + 1) * X_COUNT) // len(rest) > (j * X_COUNT) // len(rest))

    with ExitStack() as ctx:
        const = ctx.enter_context(tc.tile_pool(name="const", bufs=1))
        work = ctx.enter_context(tc.tile_pool(name="work", bufs=2))
        affp = ctx.enter_context(tc.tile_pool(name="affp", bufs=2))
        accp = ctx.enter_context(tc.tile_pool(name="accp", bufs=4))
        ps_win = ctx.enter_context(tc.psum_pool(name="ps_win", bufs=5))
        ps_aux = ctx.enter_context(tc.psum_pool(name="ps_aux", bufs=3))

        x_raw = const.tile([P, 4, HW], BF16, name="x_raw")
        wf_raw = const.tile([P, 4, C], BF16, name="wf_raw")
        wu_raw = const.tile([P, 4, C], BF16, name="wu_raw")
        chunks = [(0, 512), (512, 512), (1024, 512), (1536, 512), (2048, 256)]

        pk_a = const.tile([P, PL], BF16, name="pk_a")
        pk_b = const.tile([P, PL], BF16, name="pk_b")
        one = const.tile([P, 1], F32, name="one")
        nc.vector.memset(one[:], 1.0)
        nc.vector.memset(pk_a[:], 0.0)
        nc.gpsimd.memset(pk_b[:], 0.0)
        gam = const.tile([P, 4], BF16, name="gam")
        bet = const.tile([P, 4], BF16, name="bet")
        mea = const.tile([P, 4], BF16, name="mea")
        var = const.tile([P, 4], BF16, name="var")
        sig = const.tile([P, 1], BF16, name="sig")
        nc.scalar.dma_start(out=var[:], in_=bn_var.rearrange("(p j) -> p j", j=4))
        nc.scalar.dma_start(out=gam[:], in_=bn_gamma.rearrange("(p j) -> p j", j=4))
        nc.scalar.dma_start(out=mea[:], in_=bn_mean.rearrange("(p j) -> p j", j=4))
        nc.scalar.dma_start(out=bet[:], in_=bn_beta.rearrange("(p j) -> p j", j=4))
        nc.scalar.dma_start(out=sig[:], in_=sigma.partition_broadcast(P))

        warm = const.tile([P, 1], F32, name="warm")
        nc.scalar.activation(out=warm[:], in_=one[:], func=ACT.Sqrt)
        for dix in range(KW):
            di = dix - 3
            pk = pk_a if dix < 4 else pk_b
            s = dix if dix < 4 else dix - 4
            q_lo = max(0, PADP - IMG_W * di)
            q_hi = min(PL, HW + PADP - IMG_W * di)
            n_lo = q_lo - PADP + IMG_W * di
            n_hi = q_hi - PADP + IMG_W * di
            nc.sync.dma_start(out=pk[CP * s:CP * s + 16, q_lo:q_hi], in_=cp_v[0:16, n_lo:n_hi])
            nc.scalar.dma_start(out=pk[CP * s + 16:CP * s + CP, q_lo:q_hi], in_=cp_v[16:CP, n_lo:n_hi])

        nc.sync.dma_start(out=x_raw[:, :, 0:512], in_=x_v[:, :, 0:512])
        nc.sync.dma_start(out=wf_raw[:], in_=w_feat.rearrange("(m t) k -> m t k", t=4))
        for c0, wd in chunks[1:]:
            nc.sync.dma_start(out=x_raw[:, :, c0:c0 + wd], in_=x_v[:, :, c0:c0 + wd])
        nc.sync.dma_start(out=wu_raw[:], in_=w_fuse.rearrange("(m t) k -> m t k", t=4))

        ident_f = const.tile([P, P], F32, name="ident_f")
        masks.make_identity(nc, ident_f[:])
        ident_b = const.tile([P, P], BF16, name="ident_b")
        masks.make_identity(nc, ident_b[:])
        ident_w = ident_f

        msg = const.tile([P, 2, 4, ML // 2], MSG_DT, name="msg")
        nc.gpsimd.memset(msg[:, :, :, 0:PADM // 2], 0.0)
        nc.gpsimd.memset(msg[:, :, :, (PADM + HW) // 2:ML // 2], 0.0)

        v1 = const.tile([P, 4], F32, name="v1")
        nc.vector.tensor_scalar_add(out=v1[:], in0=var[:], scalar1=1e-5)
        sq = const.tile([P, 4], F32, name="sq")
        nc.scalar.activation(out=sq[:], in_=v1[:], func=ACT.Sqrt)
        nc.scalar.activation(out=warm[:], in_=one[:], func=ACT.Exp)
        r0 = const.tile([P, 4], F32, name="r0")
        nc.vector.reciprocal(out=r0[:], in_=sq[:])
        nt = const.tile([P, 4], F32, name="nt")
        nc.vector.tensor_tensor(out=nt[:], in0=r0[:], in1=r0[:], op=ALU.mult)
        nc.vector.tensor_tensor(out=nt[:], in0=nt[:], in1=v1[:], op=ALU.mult)
        nc.vector.tensor_scalar(out=nt[:], in0=nt[:], scalar1=-0.5, scalar2=1.5, op0=ALU.mult, op1=ALU.add)
        nc.vector.tensor_tensor(out=nt[:], in0=nt[:], in1=r0[:], op=ALU.mult)
        bn_s = const.tile([P, 4], F32, name="bn_s")
        nc.vector.tensor_tensor(out=bn_s[:], in0=nt[:], in1=gam[:], op=ALU.mult)
        bn_b = const.tile([P, 4], F32, name="bn_b")
        nc.vector.tensor_tensor(out=bn_b[:], in0=bn_s[:], in1=mea[:], op=ALU.mult)
        nc.vector.tensor_tensor(out=bn_b[:], in0=bet[:], in1=bn_b[:], op=ALU.subtract)

        sg = const.tile([P, 1], F32, name="sg")
        nc.vector.tensor_scalar_max(out=sg[:], in0=sig[:], scalar1=0.0)
        nc.vector.tensor_tensor(out=sg[:], in0=sg[:], in1=sg[:], op=ALU.mult)
        nc.vector.tensor_scalar(out=sg[:], in0=sg[:], scalar1=2.0, scalar2=1e-8, op0=ALU.mult, op1=ALU.add)
        neginv = const.tile([P, 1], F32, name="neginv")
        nc.vector.reciprocal(out=neginv[:], in_=sg[:])
        nc.vector.tensor_scalar_mul(out=neginv[:], in0=neginv[:], scalar1=-1.0)

        NT = 2 * PAIRS
        n_i = const.tile([P, NT], I32, name="n_i")
        nc.gpsimd.iota(n_i[:], pattern=[[2 * P, PAIRS], [1, 2]], base=0, channel_multiplier=2)
        thr_i = const.tile([P, IMG_W - 1], I32, name="thr_i")
        nc.gpsimd.iota(thr_i[:], pattern=[[IMG_W, IMG_W - 1]], base=IMG_W, channel_multiplier=0)
        dj_i = const.tile([P, KW], I32, name="dj_i")
        nc.gpsimd.iota(dj_i[:], pattern=[[1, KW]], base=-3, channel_multiplier=0)
        n_f = const.tile([P, NT], F32, name="n_f")
        nc.vector.tensor_copy(out=n_f[:], in_=n_i[:])
        thr_f = const.tile([P, IMG_W - 1], F32, name="thr_f")
        nc.vector.tensor_copy(out=thr_f[:], in_=thr_i[:])
        dj_f = const.tile([P, KW], F32, name="dj_f")
        nc.vector.tensor_copy(out=dj_f[:], in_=dj_i[:])
        cmp = const.tile([P, NT, IMG_W - 1], F32, name="cmp")
        nc.vector.tensor_tensor(
            out=cmp[:],
            in0=n_f[:].unsqueeze(2).to_broadcast([P, NT, IMG_W - 1]),
            in1=thr_f[:].unsqueeze(1).to_broadcast([P, NT, IMG_W - 1]),
            op=ALU.is_ge,
        )
        row = const.tile([P, NT], F32, name="row")
        nc.vector.tensor_reduce(out=row[:], in_=cmp[:], axis=AX.X, op=ALU.add)
        col = const.tile([P, NT], F32, name="col")
        nc.vector.scalar_tensor_tensor(out=col[:], in0=row[:], scalar=-48.0, in1=n_f[:], op0=ALU.mult, op1=ALU.add)
        cj = const.tile([P, NT, KW], F32, name="cj")
        nc.vector.tensor_tensor(
            out=cj[:],
            in0=col[:].unsqueeze(2).to_broadcast([P, NT, KW]),
            in1=dj_f[:].unsqueeze(1).to_broadcast([P, NT, KW]),
            op=ALU.add,
        )
        m_lo = const.tile([P, NT, KW], F32, name="m_lo")
        nc.vector.tensor_scalar(out=m_lo[:], in0=cj[:], scalar1=0.0, scalar2=None, op0=ALU.is_ge)
        mask7 = const.tile([P, NT, KW], F32, name="mask7")
        nc.vector.scalar_tensor_tensor(
            out=mask7[:].rearrange("p t j -> p (t j)"),
            in0=cj[:].rearrange("p t j -> p (t j)"),
            scalar=47.0,
            in1=m_lo[:].rearrange("p t j -> p (t j)"),
            op0=ALU.is_le,
            op1=ALU.mult,
        )
        cnt = const.tile([P, NT], F32, name="cnt")
        nc.vector.tensor_reduce(out=cnt[:], in_=mask7[:], axis=AX.X, op=ALU.add)
        nc.vector.tensor_scalar(out=cnt[:], in0=cnt[:], scalar1=-7.0, scalar2=49.0, op0=ALU.mult, op1=ALU.add)
        mask49 = const.tile([P, NT, KW, KW], F32, name="mask49")
        nc.vector.tensor_copy(out=mask49[:], in_=mask7[:].unsqueeze(3).to_broadcast([P, NT, KW, KW]))

        def prep_weight(raw, label):
            grouped = const.tile([P, 4 * C], BF16, name=label + "_grouped", align_bytes=64)
            gw = grouped[:].bitcast(F32).rearrange("p (t m u) -> p t m u", t=4, u=2)
            for half in range(2):
                ps = ps_aux.tile([P, 2, 2, P], F32, name=label + "_ps", tag="aux")
                for tt in range(2):
                    words = raw[:, 2 * half + tt, :].bitcast(F32)
                    for u in range(2):
                        nc.tensor.transpose(ps[:, tt, u, :], words[:, u::2], ident_f[:])
                nc.vector.tensor_copy(out=gw[:, 2 * half:2 * half + 2], in_=ps[:].rearrange("p t u m -> p t m u"))
            codes = const.tile([P, C], U32, name=label + "_codes", align_bytes=64)
            scl = const.tile([P, C], U8, name=label + "_scl", align_bytes=64)
            nc.vector.quantize_mx(out=codes[:].bitcast(FP8X4), scales=scl[:], in_=grouped[:])
            return codes, scl

        wf_codes, wf_scl = prep_weight(wf_raw, "wf")

        x_codes = const.tile([P, HW], U32, name="x_codes", align_bytes=64)
        x_scl = const.tile([P, HW], U8, name="x_scl", align_bytes=64)

        def stage1(k):
            c0, wd = chunks[k]
            xn = work.tile([P, 4, wd], BF16, name="xn", tag="xn", bufs=1)
            xg = work.tile([P, wd, 4], BF16, name="xg", tag="xg", align_bytes=64, bufs=1)
            for j in range(4):
                if k == 0:
                    nc.vector.tensor_scalar(
                        out=xn[:, j, :], in0=x_raw[:, j, c0:c0 + wd],
                        scalar1=bn_s[:, j:j + 1], scalar2=bn_b[:, j:j + 1], op0=ALU.mult, op1=ALU.add,
                    )
                else:
                    nc.scalar.activation(
                        out=xn[:, j, :], in_=x_raw[:, j, c0:c0 + wd], func=ACT.Identity,
                        scale=bn_s[:, j:j + 1], bias=bn_b[:, j:j + 1],
                    )
            if k == 0:
                nc.vector.tensor_copy(out=xg[:], in_=xn[:].rearrange("p j n -> p n j"))
            else:
                nc.scalar.copy(out=xg[:], in_=xn[:].rearrange("p j n -> p n j"))
            nc.vector.quantize_mx(
                out=x_codes[:, c0:c0 + wd].bitcast(FP8X4), scales=x_scl[:, c0:c0 + wd],
                in_=xg[:].rearrange("p n j -> p (n j)"),
            )
            for i in range(4 if wd == 512 else 2):
                bank = ps_win.tile([P, 2, 256], MSG_DT, name="bank", tag="win")
                for h in range(2):
                    t = i if wd == 512 else 2 * i + h
                    n0 = c0 + 256 * h if wd == 512 else c0
                    nc.tensor.matmul_mx(
                        out=bank[:, h, :],
                        lhsT=wf_codes[:, P * t:P * t + P].bitcast(FP8X4), lhsT_scale=wf_scl[:, P * t:P * t + P],
                        rhs=x_codes[:, n0:n0 + 256].bitcast(FP8X4), rhs_scale=x_scl[:, n0:n0 + 256],
                        start=True, stop=True,
                    )
                if wd == 512:
                    for e in range(2):
                        nc.scalar.copy(
                            out=msg[:, e, i, (PADM + c0) // 2:(PADM + c0) // 2 + 256],
                            in_=bank[:].rearrange("p h n -> p (h n)")[:, e::2],
                        )
                else:
                    for e in range(2):
                        nc.scalar.copy(
                            out=msg[:, e, 2 * i:2 * i + 2, (PADM + c0) // 2:(PADM + c0) // 2 + P], in_=bank[:, :, e::2],
                        )

        def affinity(pi):
            diff = affp.tile([P, 2, NOFF + 1, CP], F32, name="diff", tag="diff")
            for a in range(2):
                n0 = PADP + 2 * P * pi + a - 3
                win_a = ps_aux.tile([P, KW, P], BF16, name="win_a", tag="aux")
                win_b = ps_aux.tile([P, KW, P], BF16, name="win_b", tag="aux")
                for djx in range(KW):
                    nc.tensor.transpose(win_a[:, djx, :], pk_a[:, n0 + djx:n0 + djx + 2 * P:2], ident_b[:])
                for djx in range(KW):
                    nc.tensor.transpose(win_b[:, djx, :], pk_b[:, n0 + djx:n0 + djx + 2 * P:2], ident_b[:])
                nc.scalar.copy(out=diff[:, a, NOFF, :], in_=win_a[:, 3, 3 * CP:4 * CP])
                dv = diff[:, a, 0:NOFF, :].rearrange("p (j i) c -> p j i c", i=KW)
                centre = diff[:, a, NOFF:NOFF + 1, :].unsqueeze(1)
                nc.vector.tensor_tensor(
                    out=dv[:, :, 0:4, :], in0=win_a[:, :, 0:4 * CP].rearrange("p j (i c) -> p j i c", c=CP),
                    in1=centre.to_broadcast([P, KW, 4, CP]), op=ALU.subtract,
                )
                nc.vector.tensor_tensor(
                    out=dv[:, :, 4:7, :], in0=win_b[:, :, 0:3 * CP].rearrange("p j (i c) -> p j i c", c=CP),
                    in1=centre.to_broadcast([P, KW, 3, CP]), op=ALU.subtract,
                )
            flat = diff[:].rearrange("p a f c -> p (a f c)")
            nc.scalar.activation(out=flat, in_=flat, func=ACT.Square)
            dist = affp.tile([P, 2 * (NOFF + 1)], F32, name="dist", tag="dist")
            nc.vector.tensor_reduce(out=dist[:], in_=diff[:].rearrange("p a f c -> p (a f) c"), axis=AX.X, op=ALU.add)
            gau = affp.tile([P, 2 * (NOFF + 1)], F32, name="gau", tag="gau")
            nc.scalar.activation(out=gau[:], in_=dist[:], func=ACT.Exp, scale=neginv[:, 0:1])
            ex = affp.tile([P, 2, NOFF + 1], F32, name="ex", tag="ex")
            nc.scalar.activation(out=ex[:].rearrange("p a f -> p (a f)"), in_=gau[:], func=ACT.Exp, bias=-1.0)
            em = affp.tile([P, 2, NOFF], F32, name="em", tag="em")
            nc.gpsimd.tensor_tensor(
                out=em[:], in0=ex[:, :, 0:NOFF],
                in1=mask49[:, 2 * pi:2 * pi + 2].rearrange("p t j i -> p t (j i)"), op=ALU.mult,
            )
            zs = affp.tile([P, 2], F32, name="zs", tag="zs")
            nc.vector.tensor_reduce(out=zs[:], in_=em[:], axis=AX.X, op=ALU.add)
            zo = affp.tile([P, 2], F32, name="zo", tag="zo")
            for a in range(2):
                nc.scalar.activation(
                    out=zo[:, a:a + 1], in_=ex[:, a, NOFF:NOFF + 1], func=ACT.Identity,
                    scale=cnt[:, 2 * pi + a:2 * pi + a + 1], bias=zs[:, a:a + 1],
                )
            rz = affp.tile([P, 2], F32, name="rz", tag="rz")
            nc.vector.reciprocal(out=rz[:], in_=zo[:])
            wa = affp.tile([P, 2, NOFF], F32, name="wa", tag="wa", bufs=3)
            for a in range(2):
                nc.scalar.activation(out=wa[:, a, :], in_=em[:, a, :], func=ACT.Copy, scale=rz[:, a:a + 1])
            return wa

        def aggregate(pi, wa, hooks):
            acc_v = accp.tile([P, 2, C], F32, name="acc_v", tag="acc_v", bufs=3)
            acc_g0 = accp.tile([P, 2, C], F32, name="acc_g0", tag="acc_g")
            acc_g1 = accp.tile([P, 2, C], F32, name="acc_g1", tag="acc_g")
            acc_g = [acc_g0, acc_g1]
            parts = []
            seen_v = 0
            seen_g = 0
            for f in range(NOFF):
                for hook in hooks.get(f, []):
                    hook()
                djx, dix = divmod(f, KW)
                shift = IMG_W * (dix - 3) + (djx - 3)
                if f in x_set:
                    prod = accp.tile([P, 2, C], F32, name="xprod", tag="xprod", bufs=8)
                    parts.append(prod)
                if f in g_set:
                    if seen_g < 2:
                        prod = acc_g[seen_g]
                    else:
                        prod = accp.tile([P, 2, C], F32, name="prod", tag="prod", bufs=3)
                for a in range(2):
                    base = PADM + 2 * P * pi + a + shift
                    win = ps_win.tile([P, C], MSG_DT, name="win", tag="win")
                    for t in range(4):
                        nc.tensor.transpose(win[:, P * t:P * t + P], msg[:, base % 2, t, base // 2:base // 2 + P], ident_w[:])
                    wcol = wa[:, a, f:f + 1]
                    if f in g_set or f in x_set:
                        nc.scalar.activation(out=prod[:, a, :], in_=win[:], func=ACT.Copy, scale=wcol)
                    elif seen_v == 0:
                        nc.vector.tensor_scalar(out=acc_v[:, a, :], in0=win[:], scalar1=wcol, scalar2=None, op0=ALU.mult)
                    else:
                        nc.vector.scalar_tensor_tensor(
                            out=acc_v[:, a, :], in0=win[:], scalar=wcol, in1=acc_v[:, a, :], op0=ALU.mult, op1=ALU.add,
                        )
                if f in g_set:
                    if seen_g >= 2:
                        tgt = acc_g[seen_g % 2]
                        nc.gpsimd.tensor_tensor(out=tgt[:], in0=tgt[:], in1=prod[:], op=ALU.add)
                    seen_g += 1
                elif f not in x_set:
                    seen_v += 1
            return parts + [acc_g0, acc_g1, acc_v]

        def turn_back(parts, held, a, t):
            if a == 0 and t == 0:
                held["ag"] = work.tile([P, 2 * P, 4], BF16, name="ag", tag="ag", align_bytes=64)
            if t == 0:
                held["back"] = ps_aux.tile([P, 4, P], F32, name="back", tag="aux")
            back = held["back"]
            for i in range(len(parts)):
                nc.tensor.matmul(
                    out=back[:, t, :], lhsT=parts[i][:, a, P * t:P * t + P], rhs=ident_f[:],
                    is_transpose=True, start=(i == 0), stop=(i == len(parts) - 1),
                )
            if t == 3:
                nc.scalar.copy(
                    out=held["ag"][:].rearrange("p (n a) t -> p a n t", a=2)[:, a], in_=back[:].rearrange("p t n -> p n t"),
                )

        def stage2(pi, held):
            ag = held["ag"]
            a_codes = work.tile([P, 2 * P], U32, name="a_codes", tag="a_codes", align_bytes=64)
            a_scl = work.tile([P, 2 * P], U8, name="a_scl", tag="a_scl", align_bytes=64)
            nc.vector.quantize_mx(out=a_codes[:].bitcast(FP8X4), scales=a_scl[:], in_=ag[:].rearrange("p n t -> p (n t)"))
            o_sb = work.tile([P, 4, 2 * P], F32, name="o_sb", tag="o_sb")
            n0 = 2 * P * pi
            for u in range(2):
                ps2 = ps_aux.tile([P, 2, 2 * P], F32, name="ps2", tag="aux")
                for h in range(2):
                    t = 2 * u + h
                    nc.tensor.matmul_mx(
                        out=ps2[:, h, :],
                        lhsT=later["wu"][0][:, P * t:P * t + P].bitcast(FP8X4), lhsT_scale=later["wu"][1][:, P * t:P * t + P],
                        rhs=a_codes[:].bitcast(FP8X4), rhs_scale=a_scl[:],
                        start=True, stop=True,
                    )
                nc.vector.tensor_tensor(
                    out=o_sb[:, 2 * u:2 * u + 2, :], in0=ps2[:], in1=x_raw[:, 2 * u:2 * u + 2, n0:n0 + 2 * P], op=ALU.add,
                )
            nc.sync.dma_start(out=out_v[:, :, n0:n0 + 2 * P], in_=o_sb[:])

        later = {}

        def make_weights():
            later["wu"] = prep_weight(wu_raw, "wu")

        def make_affinity(pi):
            later["wa"] = affinity(pi)

        stage1(0)
        make_affinity(0)
        before = None
        for pi in range(PAIRS):
            wa_now = later["wa"]
            hooks = {}
            if pi == 0:
                hooks[4] = [lambda: stage1(1)]
                hooks[10] = [make_weights]
            if pi in (1, 3, 5):
                hooks[18] = [lambda k=(pi + 3) // 2: stage1(k)]
            if before is not None:
                held = {}
                for i in range(8):
                    hooks[2 * i + 1] = [lambda pp=before, hh=held, a=i // 4, t=i % 4: turn_back(pp, hh, a, t)]
                hooks[17] = [lambda q=pi - 1, hh=held: stage2(q, hh)]
            if pi + 1 < PAIRS:
                hooks[20] = [lambda q=pi + 1: make_affinity(q)]
            before = aggregate(pi, wa_now, hooks)
        held = {}
        for i in range(8):
            turn_back(before, held, i // 4, i % 4)
        stage2(PAIRS - 1, held)
